import numpy as np
import ml_dtypes


def mxq(x, axis, fmt="e4m3"):
    dtype, down = {"e4m3": (ml_dtypes.float8_e4m3fn, 7), "e5m2": (ml_dtypes.float8_e5m2, 14)}[fmt]
    v = np.moveaxis(np.asarray(x, np.float32).astype(ml_dtypes.bfloat16).astype(np.float64), axis, -1)
    blocks = v.reshape(v.shape[:-1] + (-1, 32))
    amax = np.abs(blocks).max(-1, keepdims=True)
    byte = np.maximum(np.where(amax > 0, np.frexp(amax)[1] - 1 + 127, 0) - down, 1)
    scale = np.exp2(byte - 127.0)
    codes = (blocks / scale).astype(np.float32).astype(dtype).astype(np.float64)
    return np.moveaxis((codes * scale).reshape(v.shape), -1, axis)


WIDE = False


def mx_kscale(k):
    if not WIDE:
        return np.ones(k)
    levels = np.array([10, -10, 5, -5, 0])
    a = np.random.permutation(np.resize(levels, k // 512 * 4)).reshape(k // 512, 4)
    idx = np.arange(k)
    return np.exp2(a[idx // 512, idx % 128 // 32])


BF16 = ml_dtypes.bfloat16


def bf(x):
    return np.asarray(x, np.float32).astype(BF16)


def f64(x):
    return np.asarray(x).astype(np.float64)


B, C, NH, GW, GH, GZ = 4, 512, 4, 16, 16, 8
N = GW * GH * GZ
D = C // NH
EPS = 1e-12
XS = 2.0


def l2norm(t):
    n = np.sqrt(np.sum(t * t, axis=-1, keepdims=True))
    return t / np.maximum(n, EPS)


def setup_inputs():
    s = mx_kscale(C)
    return {"x": bf(XS * np.random.standard_normal((B, C, GW, GH, GZ)) * s[None, :, None, None, None]),
            "w_q": bf(np.random.standard_normal((C, C)) / np.sqrt(C) / s[:, None]),
            "w_k": bf(np.random.standard_normal((C, C)) / np.sqrt(C) / s[:, None]),
            "temperature": bf(np.sqrt(C) * (1.0 + 0.1 * np.random.standard_normal((NH, 1, 1))))}


def reference(x, w_q, w_k, temperature):
    xt = f64(x).reshape(B, C, N).transpose(0, 2, 1)
    xq = mxq(xt, 2, "e4m3")
    q = xq @ mxq(f64(w_q), 0, "e4m3")
    k = xq @ mxq(f64(w_k), 0, "e4m3")
    q = l2norm(q.reshape(B, N, NH, D).transpose(0, 2, 3, 1))
    k = l2norm(k.reshape(B, N, NH, D).transpose(0, 2, 3, 1))
    a = (mxq(q, 3, "e4m3") @ mxq(k, 3, "e4m3").transpose(0, 1, 3, 2)) * f64(temperature)
    e = np.exp(a - a.max(-1, keepdims=True))
    return e / e.sum(-1, keepdims=True)

@@ -1,0 +1,269 @@
+from contextlib import ExitStack
+
+import concourse.mybir as mybir
+from concourse.masks import make_identity
+
+F32 = mybir.dt.float32
+BF16 = mybir.dt.bfloat16
+U32 = mybir.dt.uint32
+U8 = mybir.dt.uint8
+FP8X4 = mybir.dt.float8_e4m3fn_x4
+ACT = mybir.ActivationFunctionType
+ALU = mybir.AluOpType
+
+P = 128
+PACK = 4
+B, C, NH, D, N = 4, 512, 4, 128, 2048
+CHUNK = P * PACK
+N_CHUNKS = N // CHUNK
+PIECE = 256
+PIECES = N // PIECE
+RUN = 4
+UNITS = B * NH * 2
+EPS = 1e-12
+
+FLOPS = 2 * B * N * C * (2 * C) + 2 * B * NH * D * D * N
+
+
+def unit_of(u):
+    b, rest = divmod(u, NH * 2)
+    h, s = divmod(rest, 2)
+    return b, h, s
+
+
+def regroup(copy, grouped, rows):
+    copy(
+        out=grouped.rearrange("p (c i) j -> p c j i", i=RUN),
+        in_=rows.rearrange("p j (c i) -> p c j i", i=RUN),
+    )
+
+
+def tile_channelattention_pa_t_kernel(tc, x, w_q, w_k, temperature, out):
+    nc = tc.nc
+    x_rows = x.rearrange("b (p j) w h z -> b p j (w h z)", j=PACK)
+
+    with ExitStack() as stack:
+        keep = stack.enter_context(tc.tile_pool(name="keep", bufs=1))
+        stage = stack.enter_context(tc.tile_pool(name="stage", bufs=4))
+        units = stack.enter_context(tc.tile_pool(name="units", bufs=3))
+        words = stack.enter_context(tc.tile_pool(name="words", bufs=4))
+        soft = stack.enter_context(tc.tile_pool(name="soft", bufs=2))
+        sum_banks = stack.enter_context(tc.psum_pool(name="sum_banks", bufs=3))
+        mul_banks = stack.enter_context(tc.psum_pool(name="mul_banks", bufs=3))
+        one_bank = stack.enter_context(tc.psum_pool(name="one_bank", bufs=1))
+
+        w_raw = [keep.tile([P, PACK, C], BF16, name="w_raw%d" % s) for s in range(2)]
+        x_raw = [keep.tile([P, PACK, N], BF16, name="x_raw%d" % b) for b in range(B)]
+        temp_bf = keep.tile([P, NH], BF16, name="temp_bf")
+
+        def load_x(b):
+            for g in range(N_CHUNKS):
+                cols = slice(g * CHUNK, (g + 1) * CHUNK)
+                nc.sync.dma_start(out=x_raw[b][:, :, cols], in_=x_rows[b][:, :, cols])
+
+        nc.sync.dma_start(out=w_raw[0][:], in_=w_q.rearrange("(p j) o -> p j o", j=PACK))
+        load_x(0)
+        nc.sync.dma_start(out=w_raw[1][:], in_=w_k.rearrange("(p j) o -> p j o", j=PACK))
+        load_x(1)
+        nc.sync.dma_start(
+            out=temp_bf[:], in_=temperature.rearrange("h a c -> (h a c)").partition_broadcast(P)
+        )
+        load_x(2)
+        load_x(3)
+
+        ident = keep.tile([P, P], F32, name="ident")
+        make_identity(nc, ident[:])
+        neg_half = keep.tile([P, 1], F32, name="neg_half")
+        nc.gpsimd.memset(neg_half[:], -0.5)
+        neg_temp = keep.tile([P, NH], F32, name="neg_temp")
+        nc.vector.tensor_scalar_mul(out=neg_temp[:], in0=temp_bf[:], scalar1=-1.0)
+
+        w_codes = keep.tile([P, 2, C], U32, name="w_codes", align_bytes=64)
+        w_scales = keep.tile([P, 2, C], U8, name="w_scales", align_bytes=64)
+        x_codes = [keep.tile([P, N], U32, name="x_codes%d" % b, align_bytes=64) for b in range(B)]
+        x_scales = [keep.tile([P, N], U8, name="x_scales%d" % b, align_bytes=64) for b in range(B)]
+
+        def prepare_w(s):
+            w_grouped = stage.tile([P, C, PACK], BF16, name="w_grouped", bufs=2, align_bytes=64)
+            regroup(nc.vector.tensor_copy, w_grouped[:], w_raw[s][:])
+            nc.vector.quantize_mx(
+                out=w_codes[:, s, :].bitcast(FP8X4),
+                scales=w_scales[:, s, :],
+                in_=w_grouped[:].rearrange("p o j -> p (o j)"),
+            )
+
+        x_grouped = {}
+
+        def regroup_x(m, copy):
+            b, piece = divmod(m, PIECES)
+            cols = slice(piece * PIECE, (piece + 1) * PIECE)
+            x_grouped[m] = stage.tile([P, PIECE, PACK], BF16, name="x_grouped", align_bytes=64)
+            regroup(copy, x_grouped[m][:], x_raw[b][:, :, cols])
+
+        def quantise_x(m):
+            b, piece = divmod(m, PIECES)
+            cols = slice(piece * PIECE, (piece + 1) * PIECE)
+            nc.vector.quantize_mx(
+                out=x_codes[b][:, cols].bitcast(FP8X4),
+                scales=x_scales[b][:, cols],
+                in_=x_grouped[m][:].rearrange("p n j -> p (n j)"),
+            )
+
+        square_sum = {}
+        inv_norm = {}
+        inv_norm_row = {}
+        normed = {}
+        codes = {}
+        scales = {}
+
+        def sum_squares(u, g):
+            b, h, s = unit_of(u)
+            if g == 0:
+                square_sum[u] = units.tile([P, N_CHUNKS], F32, name="square_sum")
+            chans = slice(h * D, (h + 1) * D)
+            toks = slice(g * CHUNK, (g + 1) * CHUNK)
+            bank = sum_banks.tile([P, CHUNK], F32, name="sum_bank")
+            nc.tensor.matmul_mx(
+                out=bank[:],
+                lhsT=w_codes[:, s, chans].bitcast(FP8X4),
+                lhsT_scale=w_scales[:, s, chans],
+                rhs=x_codes[b][:, toks].bitcast(FP8X4),
+                rhs_scale=x_scales[b][:, toks],
+                start=True,
+                stop=True,
+            )
+            squares = units.tile([P, CHUNK], BF16, name="squares", bufs=2)
+            nc.scalar.activation(
+                out=squares[:], in_=bank[:], func=ACT.Square, accum_out=square_sum[u][:, g : g + 1]
+            )
+
+        def invert_norm(u):
+            halves = units.tile([P, 2], F32, name="halves")
+            nc.gpsimd.tensor_tensor(
+                out=halves[:], in0=square_sum[u][:, 0:2], in1=square_sum[u][:, 2:4], op=ALU.add
+            )
+            total = units.tile([P, 1], F32, name="total")
+            nc.gpsimd.tensor_scalar(
+                out=total[:],
+                in0=halves[:, 0:1],
+                scalar1=halves[:, 1:2],
+                scalar2=EPS * EPS,
+                op0=ALU.add,
+                op1=ALU.max,
+            )
+            inv_norm[u] = units.tile([P, 1], F32, name="inv_norm")
+            nc.gpsimd.tensor_tensor(out=inv_norm[u][:], in0=total[:], in1=neg_half[:], op=ALU.pow)
+
+        def spread_norm(u):
+            row_bank = one_bank.tile([P, D], F32, name="row_bank")
+            nc.tensor.matmul(
+                out=row_bank[:],
+                lhsT=inv_norm[u][:, 0:1].to_broadcast([P, P]),
+                rhs=ident[:],
+                start=True,
+                stop=True,
+            )
+            inv_norm_row[u] = units.tile([P, D], F32, name="inv_norm_row")
+            nc.scalar.copy(out=inv_norm_row[u][:], in_=row_bank[:])
+
+        def normalise(u, g):
+            b, h, s = unit_of(u)
+            if g == 0:
+                normed[u] = units.tile(
+                    [P, N_CHUNKS, D, PACK], BF16, name="normed", align_bytes=64
+                )
+            chans = slice(h * D, (h + 1) * D)
+            bank = mul_banks.tile([P, PACK, D], F32, name="mul_bank")
+            for t in range(PACK):
+                toks = slice(g * CHUNK + t * P, g * CHUNK + (t + 1) * P)
+                nc.tensor.matmul_mx(
+                    out=bank[:, t, :],
+                    lhsT=x_codes[b][:, toks].bitcast(FP8X4),
+                    lhsT_scale=x_scales[b][:, toks],
+                    rhs=w_codes[:, s, chans].bitcast(FP8X4),
+                    rhs_scale=w_scales[:, s, chans],
+                    start=True,
+                    stop=True,
+                )
+            nc.vector.tensor_tensor(
+                out=normed[u][:, g, :, :],
+                in0=bank[:].rearrange("p t o -> p o t"),
+                in1=inv_norm_row[u][:].unsqueeze(2).to_broadcast([P, D, PACK]),
+                op=ALU.mult,
+            )
+
+        def quantise(u):
+            codes[u] = words.tile([P, N_CHUNKS, D], U32, name="codes", align_bytes=64)
+            scales[u] = words.tile([P, N_CHUNKS, D], U8, name="scales", align_bytes=64)
+            nc.vector.quantize_mx(
+                out=codes[u][:].rearrange("p g o -> p (g o)").bitcast(FP8X4),
+                scales=scales[u][:].rearrange("p g o -> p (g o)"),
+                in_=normed[u][:].rearrange("p g o t -> p (g o t)"),
+            )
+
+        def attend(u_q, u_k):
+            b, h = unit_of(u_q)[0:2]
+            score_bank = one_bank.tile([P, D], F32, name="score_bank")
+            for g in range(N_CHUNKS):
+                nc.tensor.matmul_mx(
+                    out=score_bank[:],
+                    lhsT=codes[u_q][:, g, :].bitcast(FP8X4),
+                    lhsT_scale=scales[u_q][:, g, :],
+                    rhs=codes[u_k][:, g, :].bitcast(FP8X4),
+                    rhs_scale=scales[u_k][:, g, :],
+                    start=(g == 0),
+                    stop=(g == N_CHUNKS - 1),
+                )
+            neg_a = soft.tile([P, D], F32, name="neg_a")
+            neg_max = soft.tile([P, 1], F32, name="neg_max")
+            nc.vector.tensor_scalar(
+                out=neg_a[:],
+                in0=score_bank[:],
+                scalar1=neg_temp[:, h : h + 1],
+                scalar2=None,
+                op0=ALU.mult,
+                op1=ALU.min,
+                accum_out=neg_max[:],
+            )
+            e = soft.tile([P, D], F32, name="e")
+            e_sum = soft.tile([P, 1], F32, name="e_sum")
+            nc.scalar.activation(
+                out=e[:], in_=neg_a[:], func=ACT.Exp, scale=-1.0, bias=neg_max[:], accum_out=e_sum[:]
+            )
+            inv_sum = soft.tile([P, 1], F32, name="inv_sum")
+            nc.vector.reciprocal(out=inv_sum[:], in_=e_sum[:])
+            prob = soft.tile([P, D], F32, name="prob")
+            nc.vector.tensor_scalar_mul(out=prob[:], in0=e[:], scalar1=inv_sum[:, 0:1])
+            nc.sync.dma_start(out=out[b, h], in_=prob[:])
+
+        prepare_w(0)
+        for m in range(PIECES):
+            regroup_x(m, nc.vector.tensor_copy if m % 2 == 0 else nc.scalar.copy)
+            if m >= 1:
+                quantise_x(m - 1)
+        quantise_x(PIECES - 1)
+        prepare_w(1)
+
+        for step in range(UNITS + 3):
+            for g in range(N_CHUNKS):
+                if step < UNITS:
+                    sum_squares(step, g)
+                if 0 <= step - 2 < UNITS:
+                    normalise(step - 2, g)
+                if g == 0 and 0 <= step - 3 < UNITS:
+                    quantise(step - 3)
+                if g == 1 and 0 <= step - 1 < UNITS:
+                    spread_norm(step - 1)
+                if g == 2 and 0 <= step - 3 < UNITS and (step - 3) % 2 == 1:
+                    attend(step - 4, step - 3)
+            if step < UNITS:
+                invert_norm(step)
+            if 1 <= step <= PIECES // 2:
+                for m in (PIECES + 2 * step - 2, PIECES + 2 * step - 1):
+                    regroup_x(m, nc.vector.tensor_copy)
+                for m in (PIECES + 2 * step - 2, PIECES + 2 * step - 1):
+                    quantise_x(m)
+            if 0 <= step - 5 < 2 * PIECES:
+                quantise_x(2 * PIECES + step - 5)
+            if 0 <= step - 4 < 2 * PIECES:
+                regroup_x(2 * PIECES + step - 4, nc.scalar.copy)

@@ -43,11 +43,12 @@ def tile_channelattention_pa_t_kernel(tc, x, w_q, w_k, temperature, out):
     x_rows = x.rearrange("b (p j) w h z -> b p j (w h z)", j=PACK)
 
     with ExitStack() as stack:
+        stack.enter_context(tc.manual_schedule())
         keep = stack.enter_context(tc.tile_pool(name="keep", bufs=1))
         stage = stack.enter_context(tc.tile_pool(name="stage", bufs=4))
         units = stack.enter_context(tc.tile_pool(name="units", bufs=3))
         words = stack.enter_context(tc.tile_pool(name="words", bufs=4))
-        soft = stack.enter_context(tc.tile_pool(name="soft", bufs=2))
+        soft = stack.enter_context(tc.tile_pool(name="soft", bufs=3))
         sum_banks = stack.enter_context(tc.psum_pool(name="sum_banks", bufs=3))
         mul_banks = stack.enter_context(tc.psum_pool(name="mul_banks", bufs=3))
         one_bank = stack.enter_context(tc.psum_pool(name="one_bank", bufs=1))
@@ -61,22 +62,26 @@ def tile_channelattention_pa_t_kernel(tc, x, w_q, w_k, temperature, out):
                 cols = slice(g * CHUNK, (g + 1) * CHUNK)
                 nc.sync.dma_start(out=x_raw[b][:, :, cols], in_=x_rows[b][:, :, cols])
 
+        nc.scalar.dma_start(
+            out=temp_bf[:], in_=temperature.rearrange("h a c -> (h a c)").partition_broadcast(P)
+        )
         nc.sync.dma_start(out=w_raw[0][:], in_=w_q.rearrange("(p j) o -> p j o", j=PACK))
         load_x(0)
         nc.sync.dma_start(out=w_raw[1][:], in_=w_k.rearrange("(p j) o -> p j o", j=PACK))
-        load_x(1)
-        nc.sync.dma_start(
-            out=temp_bf[:], in_=temperature.rearrange("h a c -> (h a c)").partition_broadcast(P)
-        )
-        load_x(2)
-        load_x(3)
+        for b in range(1, B):
+            load_x(b)
 
         ident = keep.tile([P, P], F32, name="ident")
         make_identity(nc, ident[:])
         neg_half = keep.tile([P, 1], F32, name="neg_half")
         nc.gpsimd.memset(neg_half[:], -0.5)
         neg_temp = keep.tile([P, NH], F32, name="neg_temp")
-        nc.vector.tensor_scalar_mul(out=neg_temp[:], in0=temp_bf[:], scalar1=-1.0)
+        nc.gpsimd.tensor_scalar(
+            out=neg_temp[:], in0=temp_bf[:], scalar1=-1.0, scalar2=0.0, op0=ALU.mult, op1=ALU.add
+        )
+        warm = keep.tile([P, 1], F32, name="warm")
+        nc.vector.memset(warm[:], 0.0)
+        nc.scalar.activation(out=warm[:], in_=warm[:], func=ACT.Exp)
 
         w_codes = keep.tile([P, 2, C], U32, name="w_codes", align_bytes=64)
         w_scales = keep.tile([P, 2, C], U8, name="w_scales", align_bytes=64)
@@ -94,10 +99,11 @@ def tile_channelattention_pa_t_kernel(tc, x, w_q, w_k, temperature, out):
 
         x_grouped = {}
 
-        def regroup_x(m, copy):
+        def regroup_x(m):
             b, piece = divmod(m, PIECES)
             cols = slice(piece * PIECE, (piece + 1) * PIECE)
             x_grouped[m] = stage.tile([P, PIECE, PACK], BF16, name="x_grouped", align_bytes=64)
+            copy = nc.vector.tensor_copy if m % 2 == 0 else nc.scalar.copy
             regroup(copy, x_grouped[m][:], x_raw[b][:, :, cols])
 
         def quantise_x(m):
@@ -201,69 +207,100 @@ def tile_channelattention_pa_t_kernel(tc, x, w_q, w_k, temperature, out):
                 in_=normed[u][:].rearrange("p g o t -> p (g o t)"),
             )
 
-        def attend(u_q, u_k):
-            b, h = unit_of(u_q)[0:2]
+        neg_a = {}
+        neg_max = {}
+        e = {}
+        e_sum = {}
+
+        def scores(pair):
+            h = unit_of(pair)[1]
             score_bank = one_bank.tile([P, D], F32, name="score_bank")
             for g in range(N_CHUNKS):
                 nc.tensor.matmul_mx(
                     out=score_bank[:],
-                    lhsT=codes[u_q][:, g, :].bitcast(FP8X4),
-                    lhsT_scale=scales[u_q][:, g, :],
-                    rhs=codes[u_k][:, g, :].bitcast(FP8X4),
-                    rhs_scale=scales[u_k][:, g, :],
+                    lhsT=codes[pair - 1][:, g, :].bitcast(FP8X4),
+                    lhsT_scale=scales[pair - 1][:, g, :],
+                    rhs=codes[pair][:, g, :].bitcast(FP8X4),
+                    rhs_scale=scales[pair][:, g, :],
                     start=(g == 0),
                     stop=(g == N_CHUNKS - 1),
                 )
-            neg_a = soft.tile([P, D], F32, name="neg_a")
-            neg_max = soft.tile([P, 1], F32, name="neg_max")
+            neg_a[pair] = soft.tile([P, D], F32, name="neg_a")
+            neg_max[pair] = soft.tile([P, 1], F32, name="neg_max")
             nc.vector.tensor_scalar(
-                out=neg_a[:],
+                out=neg_a[pair][:],
                 in0=score_bank[:],
                 scalar1=neg_temp[:, h : h + 1],
                 scalar2=None,
                 op0=ALU.mult,
                 op1=ALU.min,
-                accum_out=neg_max[:],
+                accum_out=neg_max[pair][:],
             )
-            e = soft.tile([P, D], F32, name="e")
-            e_sum = soft.tile([P, 1], F32, name="e_sum")
+
+        def exponentials(pair):
+            e[pair] = soft.tile([P, D], F32, name="e")
+            e_sum[pair] = soft.tile([P, 1], F32, name="e_sum")
             nc.scalar.activation(
-                out=e[:], in_=neg_a[:], func=ACT.Exp, scale=-1.0, bias=neg_max[:], accum_out=e_sum[:]
+                out=e[pair][:],
+                in_=neg_a[pair][:],
+                func=ACT.Exp,
+                scale=-1.0,
+                bias=neg_max[pair][:],
+                accum_out=e_sum[pair][:],
             )
+
+        def divide_and_store(pair):
+            b, h = unit_of(pair)[0:2]
             inv_sum = soft.tile([P, 1], F32, name="inv_sum")
-            nc.vector.reciprocal(out=inv_sum[:], in_=e_sum[:])
+            nc.vector.reciprocal(out=inv_sum[:], in_=e_sum[pair][:])
             prob = soft.tile([P, D], F32, name="prob")
-            nc.vector.tensor_scalar_mul(out=prob[:], in0=e[:], scalar1=inv_sum[:, 0:1])
+            nc.gpsimd.tensor_scalar(
+                out=prob[:],
+                in0=e[pair][:],
+                scalar1=inv_sum[:, 0:1],
+                scalar2=0.0,
+                op0=ALU.mult,
+                op1=ALU.add,
+            )
             nc.sync.dma_start(out=out[b, h], in_=prob[:])
 
-        prepare_w(0)
-        for m in range(PIECES):
-            regroup_x(m, nc.vector.tensor_copy if m % 2 == 0 else nc.scalar.copy)
-            if m >= 1:
-                quantise_x(m - 1)
-        quantise_x(PIECES - 1)
-        prepare_w(1)
+        def is_pair(u):
+            return 0 <= u < UNITS and u % 2 == 1
 
-        for step in range(UNITS + 3):
+        prepare_w(0)
+        regrouped = []
+        for step in range(UNITS + 5):
             for g in range(N_CHUNKS):
+                if step == 0:
+                    for m in (2 * g, 2 * g + 1):
+                        regroup_x(m)
+                    for m in (2 * g, 2 * g + 1):
+                        quantise_x(m)
                 if step < UNITS:
                     sum_squares(step, g)
                 if 0 <= step - 2 < UNITS:
                     normalise(step - 2, g)
                 if g == 0 and 0 <= step - 3 < UNITS:
                     quantise(step - 3)
-                if g == 1 and 0 <= step - 1 < UNITS:
-                    spread_norm(step - 1)
-                if g == 2 and 0 <= step - 3 < UNITS and (step - 3) % 2 == 1:
-                    attend(step - 4, step - 3)
+                if g == 0 and is_pair(step - 5):
+                    divide_and_store(step - 5)
+                if g == 1:
+                    for m in regrouped:
+                        quantise_x(m)
+                    regrouped = []
+            if step == 0:
+                prepare_w(1)
+            if 0 <= step - 1 < UNITS:
+                spread_norm(step - 1)
             if step < UNITS:
                 invert_norm(step)
+            if is_pair(step - 3):
+                scores(step - 3)
+            if is_pair(step - 4):
+                exponentials(step - 4)
             if 1 <= step <= PIECES // 2:
-                for m in (PIECES + 2 * step - 2, PIECES + 2 * step - 1):
-                    regroup_x(m, nc.vector.tensor_copy)
-                for m in (PIECES + 2 * step - 2, PIECES + 2 * step - 1):
-                    quantise_x(m)
-            if 0 <= step - 5 < 2 * PIECES:
-                quantise_x(2 * PIECES + step - 5)
-            if 0 <= step - 4 < 2 * PIECES:
-                regroup_x(2 * PIECES + step - 4, nc.scalar.copy)
+                regrouped = [PIECES + 2 * step - 2, PIECES + 2 * step - 1]
+            elif 0 <= step - 5 < 2 * PIECES:
+                regrouped = [2 * PIECES + step - 5]
+            for m in regrouped:
+                regroup_x(m)

@@ -18,6 +18,8 @@ CHUNK = P * PACK
 N_CHUNKS = N // CHUNK
 PIECE = 256
 PIECES = N // PIECE
+V_SHARE = 64
+HALF = (V_SHARE + PIECE) // 2
 RUN = 4
 UNITS = B * NH * 2
 EPS = 1e-12
@@ -88,23 +90,30 @@ def tile_channelattention_pa_t_kernel(tc, x, w_q, w_k, temperature, out):
         x_codes = [keep.tile([P, N], U32, name="x_codes%d" % b, align_bytes=64) for b in range(B)]
         x_scales = [keep.tile([P, N], U8, name="x_scales%d" % b, align_bytes=64) for b in range(B)]
 
-        def prepare_w(s):
-            w_grouped = stage.tile([P, C, PACK], BF16, name="w_grouped", bufs=2, align_bytes=64)
-            regroup(nc.vector.tensor_copy, w_grouped[:], w_raw[s][:])
+        w_grouped = [
+            keep.tile([P, C, PACK], BF16, name="w_grouped%d" % s, align_bytes=64) for s in range(2)
+        ]
+
+        def regroup_w(s, h0, h1):
+            cols = slice(h0 * D, h1 * D)
+            regroup(nc.vector.tensor_copy, w_grouped[s][:, cols, :], w_raw[s][:, :, cols])
+
+        def quantise_w(s, h0, h1):
+            cols = slice(h0 * D, h1 * D)
             nc.vector.quantize_mx(
-                out=w_codes[:, s, :].bitcast(FP8X4),
-                scales=w_scales[:, s, :],
-                in_=w_grouped[:].rearrange("p o j -> p (o j)"),
+                out=w_codes[:, s, cols].bitcast(FP8X4),
+                scales=w_scales[:, s, cols],
+                in_=w_grouped[s][:, cols, :].rearrange("p o j -> p (o j)"),
             )
 
         x_grouped = {}
 
-        def regroup_x(m):
+        def regroup_x(copy, m, first=0, last=PIECE):
             b, piece = divmod(m, PIECES)
-            cols = slice(piece * PIECE, (piece + 1) * PIECE)
-            x_grouped[m] = stage.tile([P, PIECE, PACK], BF16, name="x_grouped", align_bytes=64)
-            copy = nc.vector.tensor_copy if m % 2 == 0 else nc.scalar.copy
-            regroup(copy, x_grouped[m][:], x_raw[b][:, :, cols])
+            if m not in x_grouped:
+                x_grouped[m] = stage.tile([P, PIECE, PACK], BF16, name="x_grouped", align_bytes=64)
+            cols = slice(piece * PIECE + first, piece * PIECE + last)
+            regroup(copy, x_grouped[m][:, first:last, :], x_raw[b][:, :, cols])
 
         def quantise_x(m):
             b, piece = divmod(m, PIECES)
@@ -198,13 +207,14 @@ def tile_channelattention_pa_t_kernel(tc, x, w_q, w_k, temperature, out):
                 op=ALU.mult,
             )
 
-        def quantise(u):
-            codes[u] = words.tile([P, N_CHUNKS, D], U32, name="codes", align_bytes=64)
-            scales[u] = words.tile([P, N_CHUNKS, D], U8, name="scales", align_bytes=64)
+        def quantise(u, g0=0, g1=N_CHUNKS):
+            if g0 == 0:
+                codes[u] = words.tile([P, N_CHUNKS, D], U32, name="codes", align_bytes=64)
+                scales[u] = words.tile([P, N_CHUNKS, D], U8, name="scales", align_bytes=64)
             nc.vector.quantize_mx(
-                out=codes[u][:].rearrange("p g o -> p (g o)").bitcast(FP8X4),
-                scales=scales[u][:].rearrange("p g o -> p (g o)"),
-                in_=normed[u][:].rearrange("p g o t -> p (g o t)"),
+                out=codes[u][:, g0:g1, :].rearrange("p g o -> p (g o)").bitcast(FP8X4),
+                scales=scales[u][:, g0:g1, :].rearrange("p g o -> p (g o)"),
+                in_=normed[u][:, g0:g1, :, :].rearrange("p g o t -> p (g o t)"),
             )
 
         neg_a = {}
@@ -267,40 +277,77 @@ def tile_channelattention_pa_t_kernel(tc, x, w_q, w_k, temperature, out):
         def is_pair(u):
             return 0 <= u < UNITS and u % 2 == 1
 
-        prepare_w(0)
-        regrouped = []
+        on_vector = nc.vector.tensor_copy
+        on_scalar = nc.scalar.copy
+
+        regroup_w(0, 0, 1)
+        regroup_x(on_vector, 0)
+        regroup_x(on_scalar, 1)
+        quantise_w(0, 0, 1)
+        quantise_x(0)
+        regroup_x(on_vector, 2)
+        regroup_x(on_scalar, 3)
+        quantise_x(1)
+        quantise_x(2)
+        regroup_x(on_vector, 4)
+        regroup_x(on_scalar, 5)
+        quantise_x(3)
+        quantise_x(4)
+        regroup_x(on_vector, 6)
+        regroup_x(on_vector, 7)
+        quantise_x(5)
+        quantise_x(6)
+        regroup_w(1, 0, 1)
+        quantise_x(7)
+
+        regroup_w(0, 1, NH)
+        quantise_w(1, 0, 1)
+        regroup_w(1, 1, NH)
+        quantise_w(0, 1, 2)
+        quantise_w(0, 2, NH)
+        quantise_w(1, 1, 2)
+        quantise_w(1, 2, NH)
+
+        in_step = {}
+        for m in range(PIECES, B * PIECES):
+            if m < 2 * PIECES:
+                at = 1 + (m - PIECES) * 6 // PIECES
+            else:
+                at = m - PIECES - 1
+            in_step.setdefault(at, []).append(m)
+
         for step in range(UNITS + 5):
+            todo = in_step.get(step, [])
             for g in range(N_CHUNKS):
-                if step == 0:
-                    for m in (2 * g, 2 * g + 1):
-                        regroup_x(m)
-                    for m in (2 * g, 2 * g + 1):
-                        quantise_x(m)
                 if step < UNITS:
                     sum_squares(step, g)
                 if 0 <= step - 2 < UNITS:
                     normalise(step - 2, g)
-                if g == 0 and 0 <= step - 3 < UNITS:
+                if g == 0 and 0 <= step - 3 < UNITS - 1:
                     quantise(step - 3)
                 if g == 0 and is_pair(step - 5):
                     divide_and_store(step - 5)
                 if g == 1:
-                    for m in regrouped:
+                    for m in in_step.get(step - 1, []):
                         quantise_x(m)
-                    regrouped = []
-            if step == 0:
-                prepare_w(1)
-            if 0 <= step - 1 < UNITS:
-                spread_norm(step - 1)
+                    for m in todo:
+                        regroup_x(on_scalar, m, V_SHARE, HALF)
+                if g == 2:
+                    for m in todo:
+                        regroup_x(on_vector, m, 0, V_SHARE)
+                    if 0 <= step - 1 < UNITS:
+                        spread_norm(step - 1)
+                    if step - 2 == UNITS - 1:
+                        quantise(step - 2, 0, 2)
+                if g == 3:
+                    for m in todo:
+                        regroup_x(on_scalar, m, HALF, PIECE)
+            if step - 2 == UNITS - 1:
+                quantise(step - 2, 2, 3)
+                quantise(step - 2, 3, 4)
             if step < UNITS:
                 invert_norm(step)
             if is_pair(step - 3):
                 scores(step - 3)
             if is_pair(step - 4):
                 exponentials(step - 4)
-            if 1 <= step <= PIECES // 2:
-                regrouped = [PIECES + 2 * step - 2, PIECES + 2 * step - 1]
-            elif 0 <= step - 5 < 2 * PIECES:
-                regrouped = [2 * PIECES + step - 5]
-            for m in regrouped:
-                regroup_x(m)

@@ -335,16 +335,15 @@ def tile_channelattention_pa_t_kernel(tc, x, w_q, w_k, temperature, out):
                 if g == 2:
                     for m in todo:
                         regroup_x(on_vector, m, 0, V_SHARE)
-                    if 0 <= step - 1 < UNITS:
-                        spread_norm(step - 1)
                     if step - 2 == UNITS - 1:
                         quantise(step - 2, 0, 2)
-                if g == 3:
-                    for m in todo:
-                        regroup_x(on_scalar, m, HALF, PIECE)
             if step - 2 == UNITS - 1:
                 quantise(step - 2, 2, 3)
                 quantise(step - 2, 3, 4)
+            if 0 <= step - 1 < UNITS:
+                spread_norm(step - 1)
+            for m in todo:
+                regroup_x(on_scalar, m, HALF, PIECE)
             if step < UNITS:
                 invert_norm(step)
             if is_pair(step - 3):

@@ -20,6 +20,8 @@ PIECE = 256
 PIECES = N // PIECE
 V_SHARE = 64
 HALF = (V_SHARE + PIECE) // 2
+HEAD_PIECES = 4
+LAG = 10
 RUN = 4
 UNITS = B * NH * 2
 EPS = 1e-12
@@ -308,45 +310,46 @@ def tile_channelattention_pa_t_kernel(tc, x, w_q, w_k, temperature, out):
         quantise_w(1, 1, 2)
         quantise_w(1, 2, NH)
 
-        in_step = {}
-        for m in range(PIECES, B * PIECES):
-            if m < 2 * PIECES:
-                at = 1 + (m - PIECES) * 6 // PIECES
-            else:
-                at = m - PIECES - 1
-            in_step.setdefault(at, []).append(m)
+        for m in range(PIECES, PIECES + HEAD_PIECES):
+            regroup_x(on_vector, m)
+            if m > PIECES:
+                quantise_x(m - 1)
+        quantise_x(PIECES + HEAD_PIECES - 1)
 
-        for step in range(UNITS + 5):
-            todo = in_step.get(step, [])
-            for g in range(N_CHUNKS):
-                if step < UNITS:
-                    sum_squares(step, g)
-                if 0 <= step - 2 < UNITS:
-                    normalise(step - 2, g)
-                if g == 0 and 0 <= step - 3 < UNITS - 1:
-                    quantise(step - 3)
-                if g == 0 and is_pair(step - 5):
-                    divide_and_store(step - 5)
-                if g == 1:
-                    for m in in_step.get(step - 1, []):
-                        quantise_x(m)
-                    for m in todo:
-                        regroup_x(on_scalar, m, V_SHARE, HALF)
-                if g == 2:
-                    for m in todo:
-                        regroup_x(on_vector, m, 0, V_SHARE)
-                    if step - 2 == UNITS - 1:
-                        quantise(step - 2, 0, 2)
-            if step - 2 == UNITS - 1:
-                quantise(step - 2, 2, 3)
-                quantise(step - 2, 3, 4)
-            if 0 <= step - 1 < UNITS:
-                spread_norm(step - 1)
-            for m in todo:
-                regroup_x(on_scalar, m, HALF, PIECE)
-            if step < UNITS:
-                invert_norm(step)
-            if is_pair(step - 3):
-                scores(step - 3)
-            if is_pair(step - 4):
-                exponentials(step - 4)
+        first = PIECES + HEAD_PIECES
+        in_slot = {}
+        for m in range(first, B * PIECES):
+            in_slot[N_CHUNKS * (1 + (m - first) * 22 // (B * PIECES - first)) + 1] = m
+
+        for slot in range(N_CHUNKS * UNITS + LAG + 4 * N_CHUNKS):
+            u, g = divmod(slot, N_CHUNKS)
+            if u < UNITS:
+                sum_squares(u, g)
+            v, k = divmod(slot - LAG, N_CHUNKS)
+            if 0 <= v < UNITS:
+                normalise(v, k)
+            if k == 0 and 0 <= v - 1 < UNITS - 1:
+                quantise(v - 1)
+            if k == 2 and v == UNITS - 1:
+                quantise(v, 0, 2)
+            if k == 3 and v == UNITS - 1:
+                quantise(v, 2, 3)
+                quantise(v, 3, 4)
+            if k == 0 and is_pair(v - 3):
+                divide_and_store(v - 3)
+            if slot in in_slot:
+                regroup_x(on_scalar, in_slot[slot], V_SHARE, HALF)
+            if slot - 1 in in_slot:
+                regroup_x(on_vector, in_slot[slot - 1], 0, V_SHARE)
+            if k == 3 and 0 <= v + 1 < UNITS:
+                spread_norm(v + 1)
+            if slot - 2 in in_slot:
+                regroup_x(on_scalar, in_slot[slot - 2], HALF, PIECE)
+            if slot - 4 in in_slot:
+                quantise_x(in_slot[slot - 4])
+            if g == 3 and u < UNITS:
+                invert_norm(u)
+            if k == 3 and is_pair(v - 1):
+                scores(v - 1)
+            if k == 3 and is_pair(v - 2):
+                exponentials(v - 2)

@@ -20,8 +20,8 @@ PIECE = 256
 PIECES = N // PIECE
 V_SHARE = 64
 HALF = (V_SHARE + PIECE) // 2
-HEAD_PIECES = 4
-LAG = 10
+HEAD_PIECES = 2
+LAG = 8
 RUN = 4
 UNITS = B * NH * 2
 EPS = 1e-12
@@ -58,13 +58,16 @@ def tile_channelattention_pa_t_kernel(tc, x, w_q, w_k, temperature, out):
         one_bank = stack.enter_context(tc.psum_pool(name="one_bank", bufs=1))
 
         w_raw = [keep.tile([P, PACK, C], BF16, name="w_raw%d" % s) for s in range(2)]
-        x_raw = [keep.tile([P, PACK, N], BF16, name="x_raw%d" % b) for b in range(B)]
+        x_raw = [
+            [keep.tile([P, PACK, CHUNK], BF16, name="x_raw%d_%d" % (b, g)) for g in range(N_CHUNKS)]
+            for b in range(B)
+        ]
         temp_bf = keep.tile([P, NH], BF16, name="temp_bf")
 
         def load_x(b):
             for g in range(N_CHUNKS):
                 cols = slice(g * CHUNK, (g + 1) * CHUNK)
-                nc.sync.dma_start(out=x_raw[b][:, :, cols], in_=x_rows[b][:, :, cols])
+                nc.sync.dma_start(out=x_raw[b][g][:], in_=x_rows[b][:, :, cols])
 
         nc.scalar.dma_start(
             out=temp_bf[:], in_=temperature.rearrange("h a c -> (h a c)").partition_broadcast(P)
@@ -114,8 +117,9 @@ def tile_channelattention_pa_t_kernel(tc, x, w_q, w_k, temperature, out):
             b, piece = divmod(m, PIECES)
             if m not in x_grouped:
                 x_grouped[m] = stage.tile([P, PIECE, PACK], BF16, name="x_grouped", align_bytes=64)
-            cols = slice(piece * PIECE + first, piece * PIECE + last)
-            regroup(copy, x_grouped[m][:, first:last, :], x_raw[b][:, :, cols])
+            g, start = divmod(piece * PIECE, CHUNK)
+            cols = slice(start + first, start + last)
+            regroup(copy, x_grouped[m][:, first:last, :], x_raw[b][g][:, :, cols])
 
         def quantise_x(m):
             b, piece = divmod(m, PIECES)
@@ -319,7 +323,7 @@ def tile_channelattention_pa_t_kernel(tc, x, w_q, w_k, temperature, out):
         first = PIECES + HEAD_PIECES
         in_slot = {}
         for m in range(first, B * PIECES):
-            in_slot[N_CHUNKS * (1 + (m - first) * 22 // (B * PIECES - first)) + 1] = m
+            in_slot[N_CHUNKS * (1 + m - first) + 1] = m
 
         for slot in range(N_CHUNKS * UNITS + LAG + 4 * N_CHUNKS):
             u, g = divmod(slot, N_CHUNKS)

@@ -16,11 +16,16 @@ PACK = 4
 B, C, NH, D, N = 4, 512, 4, 128, 2048
 CHUNK = P * PACK
 N_CHUNKS = N // CHUNK
+FIRST = 128
 PIECE = 256
 PIECES = N // PIECE
 V_SHARE = 64
 HALF = (V_SHARE + PIECE) // 2
 HEAD_PIECES = 2
+SUM_AT, SPREAD_AT, INVERT_AT = 4, 6, 6
+QUANTISE_AT = 0
+SUM_BANKS, MUL_BANKS = 4, 4
+SCORES_AT, SCALE_AT = 2, 3
 LAG = 8
 RUN = 4
 UNITS = B * NH * 2
@@ -52,12 +57,11 @@ def tile_channelattention_pa_t_kernel(tc, x, w_q, w_k, temperature, out):
         stage = stack.enter_context(tc.tile_pool(name="stage", bufs=4))
         units = stack.enter_context(tc.tile_pool(name="units", bufs=3))
         words = stack.enter_context(tc.tile_pool(name="words", bufs=4))
-        soft = stack.enter_context(tc.tile_pool(name="soft", bufs=3))
-        sum_banks = stack.enter_context(tc.psum_pool(name="sum_banks", bufs=3))
-        mul_banks = stack.enter_context(tc.psum_pool(name="mul_banks", bufs=3))
-        one_bank = stack.enter_context(tc.psum_pool(name="one_bank", bufs=1))
+        sum_banks = stack.enter_context(tc.psum_pool(name="sum_banks", bufs=SUM_BANKS))
+        mul_banks = stack.enter_context(tc.psum_pool(name="mul_banks", bufs=MUL_BANKS))
 
         w_raw = [keep.tile([P, PACK, C], BF16, name="w_raw%d" % s) for s in range(2)]
+        w_first = keep.tile([P, PACK, FIRST], BF16, name="w_first")
         x_raw = [
             [keep.tile([P, PACK, CHUNK], BF16, name="x_raw%d_%d" % (b, g)) for g in range(N_CHUNKS)]
             for b in range(B)
@@ -72,23 +76,23 @@ def tile_channelattention_pa_t_kernel(tc, x, w_q, w_k, temperature, out):
         nc.scalar.dma_start(
             out=temp_bf[:], in_=temperature.rearrange("h a c -> (h a c)").partition_broadcast(P)
         )
-        nc.sync.dma_start(out=w_raw[0][:], in_=w_q.rearrange("(p j) o -> p j o", j=PACK))
+        w_rows = [w.rearrange("(p j) o -> p j o", j=PACK) for w in (w_q, w_k)]
+        nc.sync.dma_start(out=w_first[:], in_=w_rows[0][:, :, 0:FIRST])
         load_x(0)
-        nc.sync.dma_start(out=w_raw[1][:], in_=w_k.rearrange("(p j) o -> p j o", j=PACK))
+        nc.sync.dma_start(out=w_raw[0][:, :, FIRST:C], in_=w_rows[0][:, :, FIRST:C])
+        nc.sync.dma_start(out=w_raw[1][:], in_=w_rows[1])
         for b in range(1, B):
             load_x(b)
 
         ident = keep.tile([P, P], F32, name="ident")
         make_identity(nc, ident[:])
-        neg_half = keep.tile([P, 1], F32, name="neg_half")
-        nc.gpsimd.memset(neg_half[:], -0.5)
         neg_temp = keep.tile([P, NH], F32, name="neg_temp")
         nc.gpsimd.tensor_scalar(
             out=neg_temp[:], in0=temp_bf[:], scalar1=-1.0, scalar2=0.0, op0=ALU.mult, op1=ALU.add
         )
         warm = keep.tile([P, 1], F32, name="warm")
-        nc.vector.memset(warm[:], 0.0)
-        nc.scalar.activation(out=warm[:], in_=warm[:], func=ACT.Exp)
+        nc.vector.memset(warm[:], 1.0)
+        nc.scalar.activation(out=warm[:], in_=warm[:], func=ACT.Abs_reciprocal_sqrt)
 
         w_codes = keep.tile([P, 2, C], U32, name="w_codes", align_bytes=64)
         w_scales = keep.tile([P, 2, C], U8, name="w_scales", align_bytes=64)
@@ -101,7 +105,8 @@ def tile_channelattention_pa_t_kernel(tc, x, w_q, w_k, temperature, out):
 
         def regroup_w(s, h0, h1):
             cols = slice(h0 * D, h1 * D)
-            regroup(nc.vector.tensor_copy, w_grouped[s][:, cols, :], w_raw[s][:, :, cols])
+            rows = w_first if s == 0 and h1 * D <= FIRST else w_raw[s]
+            regroup(nc.vector.tensor_copy, w_grouped[s][:, cols, :], rows[:, :, cols])
 
         def quantise_w(s, h0, h1):
             cols = slice(h0 * D, h1 * D)
@@ -131,7 +136,7 @@ def tile_channelattention_pa_t_kernel(tc, x, w_q, w_k, temperature, out):
             )
 
         square_sum = {}
-        inv_norm = {}
+        total = {}
         inv_norm_row = {}
         normed = {}
         codes = {}
@@ -158,34 +163,25 @@ def tile_channelattention_pa_t_kernel(tc, x, w_q, w_k, temperature, out):
                 out=squares[:], in_=bank[:], func=ACT.Square, accum_out=square_sum[u][:, g : g + 1]
             )
 
-        def invert_norm(u):
-            halves = units.tile([P, 2], F32, name="halves")
-            nc.gpsimd.tensor_tensor(
-                out=halves[:], in0=square_sum[u][:, 0:2], in1=square_sum[u][:, 2:4], op=ALU.add
+        def add_squares(u):
+            sums = units.tile([P, N_CHUNKS], F32, name="sums")
+            total[u] = units.tile([P, 1], F32, name="total")
+            nc.scalar.activation(
+                out=sums[:], in_=square_sum[u][:], func=ACT.Copy, accum_out=total[u][:]
             )
-            total = units.tile([P, 1], F32, name="total")
-            nc.gpsimd.tensor_scalar(
-                out=total[:],
-                in0=halves[:, 0:1],
-                scalar1=halves[:, 1:2],
-                scalar2=EPS * EPS,
-                op0=ALU.add,
-                op1=ALU.max,
-            )
-            inv_norm[u] = units.tile([P, 1], F32, name="inv_norm")
-            nc.gpsimd.tensor_tensor(out=inv_norm[u][:], in0=total[:], in1=neg_half[:], op=ALU.pow)
 
-        def spread_norm(u):
-            row_bank = one_bank.tile([P, D], F32, name="row_bank")
-            nc.tensor.matmul(
-                out=row_bank[:],
-                lhsT=inv_norm[u][:, 0:1].to_broadcast([P, P]),
-                rhs=ident[:],
-                start=True,
-                stop=True,
-            )
+        row_bank = {}
+
+        def spread_sum(u):
+            bank = sum_banks.tile([P, CHUNK], F32, name="sum_bank")
+            row_bank[u] = bank[:, 0:D]
+            nc.tensor.transpose(row_bank[u], total[u][:, 0:1].to_broadcast([P, P]), ident[:])
+
+        def invert_norm(u):
             inv_norm_row[u] = units.tile([P, D], F32, name="inv_norm_row")
-            nc.scalar.copy(out=inv_norm_row[u][:], in_=row_bank[:])
+            nc.scalar.activation(
+                out=inv_norm_row[u][:], in_=row_bank[u], func=ACT.Abs_reciprocal_sqrt
+            )
 
         def normalise(u, g):
             b, h, s = unit_of(u)
@@ -206,11 +202,13 @@ def tile_channelattention_pa_t_kernel(tc, x, w_q, w_k, temperature, out):
                     start=True,
                     stop=True,
                 )
-            nc.vector.tensor_tensor(
+            nc.vector.scalar_tensor_tensor(
                 out=normed[u][:, g, :, :],
-                in0=bank[:].rearrange("p t o -> p o t"),
-                in1=inv_norm_row[u][:].unsqueeze(2).to_broadcast([P, D, PACK]),
-                op=ALU.mult,
+                in0=inv_norm_row[u][:].unsqueeze(2).to_broadcast([P, D, PACK]),
+                scalar=1.0 / EPS,
+                in1=bank[:].rearrange("p t o -> p o t"),
+                op0=ALU.min,
+                op1=ALU.mult,
             )
 
         def quantise(u, g0=0, g1=N_CHUNKS):
@@ -223,17 +221,22 @@ def tile_channelattention_pa_t_kernel(tc, x, w_q, w_k, temperature, out):
                 in_=normed[u][:, g0:g1, :, :].rearrange("p g o t -> p (g o t)"),
             )
 
-        neg_a = {}
-        neg_max = {}
-        e = {}
-        e_sum = {}
+        HEADS = B * NH
+        neg_a = keep.tile([P, HEADS, D], F32, name="neg_a")
+        neg_max = keep.tile([P, HEADS], F32, name="neg_max")
+        e = keep.tile([P, HEADS, D], F32, name="e")
+        e_sum = keep.tile([P, HEADS], F32, name="e_sum")
+        inv_sum = keep.tile([P, HEADS], F32, name="inv_sum")
+        prob = keep.tile([P, HEADS, D], F32, name="prob")
+
+        score_bank = {}
 
         def scores(pair):
-            h = unit_of(pair)[1]
-            score_bank = one_bank.tile([P, D], F32, name="score_bank")
+            bank = mul_banks.tile([P, PACK, D], F32, name="mul_bank")
+            score_bank[pair] = bank[:, 0, :]
             for g in range(N_CHUNKS):
                 nc.tensor.matmul_mx(
-                    out=score_bank[:],
+                    out=score_bank[pair],
                     lhsT=codes[pair - 1][:, g, :].bitcast(FP8X4),
                     lhsT_scale=scales[pair - 1][:, g, :],
                     rhs=codes[pair][:, g, :].bitcast(FP8X4),
@@ -241,44 +244,46 @@ def tile_channelattention_pa_t_kernel(tc, x, w_q, w_k, temperature, out):
                     start=(g == 0),
                     stop=(g == N_CHUNKS - 1),
                 )
-            neg_a[pair] = soft.tile([P, D], F32, name="neg_a")
-            neg_max[pair] = soft.tile([P, 1], F32, name="neg_max")
+
+        def scale_scores(pair):
+            h = unit_of(pair)[1]
             nc.vector.tensor_scalar(
-                out=neg_a[pair][:],
-                in0=score_bank[:],
+                out=neg_a[:, pair // 2, :],
+                in0=score_bank[pair],
                 scalar1=neg_temp[:, h : h + 1],
                 scalar2=None,
                 op0=ALU.mult,
                 op1=ALU.min,
-                accum_out=neg_max[pair][:],
+                accum_out=neg_max[:, pair // 2 : pair // 2 + 1],
             )
 
-        def exponentials(pair):
-            e[pair] = soft.tile([P, D], F32, name="e")
-            e_sum[pair] = soft.tile([P, 1], F32, name="e_sum")
+        def exponentials(head):
             nc.scalar.activation(
-                out=e[pair][:],
-                in_=neg_a[pair][:],
+                out=e[:, head, :],
+                in_=neg_a[:, head, :],
                 func=ACT.Exp,
                 scale=-1.0,
-                bias=neg_max[pair][:],
-                accum_out=e_sum[pair][:],
+                bias=neg_max[:, head : head + 1],
+                accum_out=e_sum[:, head : head + 1],
             )
 
-        def divide_and_store(pair):
-            b, h = unit_of(pair)[0:2]
-            inv_sum = soft.tile([P, 1], F32, name="inv_sum")
-            nc.vector.reciprocal(out=inv_sum[:], in_=e_sum[pair][:])
-            prob = soft.tile([P, D], F32, name="prob")
-            nc.gpsimd.tensor_scalar(
-                out=prob[:],
-                in0=e[pair][:],
-                scalar1=inv_sum[:, 0:1],
-                scalar2=0.0,
+        def invert_sums(h0, h1):
+            nc.vector.reciprocal(out=inv_sum[:, h0:h1], in_=e_sum[:, h0:h1])
+
+        def divide(head):
+            nc.vector.tensor_scalar(
+                out=prob[:, head, :],
+                in0=e[:, head, :],
+                scalar1=inv_sum[:, head : head + 1],
+                scalar2=None,
                 op0=ALU.mult,
-                op1=ALU.add,
             )
-            nc.sync.dma_start(out=out[b, h], in_=prob[:])
+
+        def store(h0, h1):
+            b, h = divmod(h0, NH)
+            nc.sync.dma_start(
+                out=out[b, h : h + h1 - h0].rearrange("h i j -> i h j"), in_=prob[:, h0:h1, :]
+            )
 
         def is_pair(u):
             return 0 <= u < UNITS and u % 2 == 1
@@ -300,7 +305,7 @@ def tile_channelattention_pa_t_kernel(tc, x, w_q, w_k, temperature, out):
         quantise_x(3)
         quantise_x(4)
         regroup_x(on_vector, 6)
-        regroup_x(on_vector, 7)
+        regroup_x(on_scalar, 7)
         quantise_x(5)
         quantise_x(6)
         regroup_w(1, 0, 1)
@@ -325,35 +330,62 @@ def tile_channelattention_pa_t_kernel(tc, x, w_q, w_k, temperature, out):
         for m in range(first, B * PIECES):
             in_slot[N_CHUNKS * (1 + m - first) + 1] = m
 
-        for slot in range(N_CHUNKS * UNITS + LAG + 4 * N_CHUNKS):
+        last = UNITS - 1
+        for slot in range(N_CHUNKS * UNITS + LAG):
             u, g = divmod(slot, N_CHUNKS)
             if u < UNITS:
                 sum_squares(u, g)
+            w, r = divmod(slot - SUM_AT, N_CHUNKS)
+            if r == 0 and 0 <= w < UNITS:
+                add_squares(w)
             v, k = divmod(slot - LAG, N_CHUNKS)
             if 0 <= v < UNITS:
                 normalise(v, k)
-            if k == 0 and 0 <= v - 1 < UNITS - 1:
+            w, r = divmod(slot - SPREAD_AT, N_CHUNKS)
+            if r == 0 and 0 <= w < UNITS:
+                spread_sum(w)
+            w, r = divmod(slot - INVERT_AT, N_CHUNKS)
+            if r == 0 and 0 <= w < UNITS:
+                invert_norm(w)
+            if k == QUANTISE_AT and 0 <= v - 1 < last:
                 quantise(v - 1)
-            if k == 2 and v == UNITS - 1:
+            if k == 2 and v == last:
                 quantise(v, 0, 2)
-            if k == 3 and v == UNITS - 1:
+            if k == 3 and v == last:
                 quantise(v, 2, 3)
                 quantise(v, 3, 4)
-            if k == 0 and is_pair(v - 3):
-                divide_and_store(v - 3)
             if slot in in_slot:
                 regroup_x(on_scalar, in_slot[slot], V_SHARE, HALF)
             if slot - 1 in in_slot:
                 regroup_x(on_vector, in_slot[slot - 1], 0, V_SHARE)
-            if k == 3 and 0 <= v + 1 < UNITS:
-                spread_norm(v + 1)
             if slot - 2 in in_slot:
                 regroup_x(on_scalar, in_slot[slot - 2], HALF, PIECE)
             if slot - 4 in in_slot:
                 quantise_x(in_slot[slot - 4])
-            if g == 3 and u < UNITS:
-                invert_norm(u)
-            if k == 3 and is_pair(v - 1):
+            if k == SCORES_AT and is_pair(v - 1):
                 scores(v - 1)
-            if k == 3 and is_pair(v - 2):
-                exponentials(v - 2)
+            if k == SCALE_AT and is_pair(v - 1):
+                scale_scores(v - 1)
+            if slot == N_CHUNKS * last + INVERT_AT:
+                for head in range(HEADS - 2):
+                    exponentials(head)
+            if slot == N_CHUNKS * last + LAG:
+                exponentials(HEADS - 2)
+
+        scores(last)
+        invert_sums(0, HEADS - 1)
+        for head in range(2 * NH):
+            divide(head)
+        store(0, NH)
+        store(NH, 2 * NH)
+        scale_scores(last)
+        exponentials(HEADS - 1)
+        for head in range(2 * NH, 3 * NH):
+            divide(head)
+        store(2 * NH, 3 * NH)
+        invert_sums(HEADS - 1, HEADS)
+        divide(HEADS - 1)
+        store(HEADS - 1, HEADS)
+        for head in range(3 * NH, HEADS - 1):
+            divide(head)
+        store(3 * NH, HEADS - 1)

@@ -19,13 +19,16 @@ N_CHUNKS = N // CHUNK
 FIRST = 128
 PIECE = 256
 PIECES = N // PIECE
-V_SHARE = 64
-HALF = (V_SHARE + PIECE) // 2
+G_SHARE = 128
+V_SHARE = 0
 HEAD_PIECES = 2
+FIRST_LATER = PIECES + HEAD_PIECES
+FIRST_SLOT = 5
+X_BUFS = 2
 SUM_AT, SPREAD_AT, INVERT_AT = 4, 6, 6
 QUANTISE_AT = 0
 SUM_BANKS, MUL_BANKS = 4, 4
-SCORES_AT, SCALE_AT = 2, 3
+SCORES_AT, SCALE_AT = 8, 9
 LAG = 8
 RUN = 4
 UNITS = B * NH * 2
@@ -54,7 +57,8 @@ def tile_channelattention_pa_t_kernel(tc, x, w_q, w_k, temperature, out):
     with ExitStack() as stack:
         stack.enter_context(tc.manual_schedule())
         keep = stack.enter_context(tc.tile_pool(name="keep", bufs=1))
-        stage = stack.enter_context(tc.tile_pool(name="stage", bufs=4))
+        head = stack.enter_context(tc.tile_pool(name="head", bufs=4))
+        stage = stack.enter_context(tc.tile_pool(name="stage", bufs=X_BUFS))
         units = stack.enter_context(tc.tile_pool(name="units", bufs=3))
         words = stack.enter_context(tc.tile_pool(name="words", bufs=4))
         sum_banks = stack.enter_context(tc.psum_pool(name="sum_banks", bufs=SUM_BANKS))
@@ -103,10 +107,26 @@ def tile_channelattention_pa_t_kernel(tc, x, w_q, w_k, temperature, out):
             keep.tile([P, C, PACK], BF16, name="w_grouped%d" % s, align_bytes=64) for s in range(2)
         ]
 
+        def on_vector(grouped, rows):
+            regroup(nc.vector.tensor_copy, grouped, rows)
+
+        def on_scalar(grouped, rows):
+            regroup(nc.scalar.copy, grouped, rows)
+
+        def on_gpsimd(grouped, rows):
+            nc.gpsimd.tensor_scalar(
+                out=grouped,
+                in0=rows.rearrange("p j w -> p w j"),
+                scalar1=1.0,
+                scalar2=0.0,
+                op0=ALU.mult,
+                op1=ALU.add,
+            )
+
         def regroup_w(s, h0, h1):
             cols = slice(h0 * D, h1 * D)
             rows = w_first if s == 0 and h1 * D <= FIRST else w_raw[s]
-            regroup(nc.vector.tensor_copy, w_grouped[s][:, cols, :], rows[:, :, cols])
+            on_vector(w_grouped[s][:, cols, :], rows[:, :, cols])
 
         def quantise_w(s, h0, h1):
             cols = slice(h0 * D, h1 * D)
@@ -121,10 +141,15 @@ def tile_channelattention_pa_t_kernel(tc, x, w_q, w_k, temperature, out):
         def regroup_x(copy, m, first=0, last=PIECE):
             b, piece = divmod(m, PIECES)
             if m not in x_grouped:
-                x_grouped[m] = stage.tile([P, PIECE, PACK], BF16, name="x_grouped", align_bytes=64)
+                if m < FIRST_LATER:
+                    x_grouped[m] = head.tile([P, PIECE, PACK], BF16, name="x_head", align_bytes=64)
+                else:
+                    x_grouped[m] = stage.tile(
+                        [P, PIECE, PACK], BF16, name="x_grouped", align_bytes=64
+                    )
             g, start = divmod(piece * PIECE, CHUNK)
             cols = slice(start + first, start + last)
-            regroup(copy, x_grouped[m][:, first:last, :], x_raw[b][g][:, :, cols])
+            copy(x_grouped[m][:, first:last, :], x_raw[b][g][:, :, cols])
 
         def quantise_x(m):
             b, piece = divmod(m, PIECES)
@@ -288,8 +313,6 @@ def tile_channelattention_pa_t_kernel(tc, x, w_q, w_k, temperature, out):
         def is_pair(u):
             return 0 <= u < UNITS and u % 2 == 1
 
-        on_vector = nc.vector.tensor_copy
-        on_scalar = nc.scalar.copy
 
         regroup_w(0, 0, 1)
         regroup_x(on_vector, 0)
@@ -328,9 +351,11 @@ def tile_channelattention_pa_t_kernel(tc, x, w_q, w_k, temperature, out):
         first = PIECES + HEAD_PIECES
         in_slot = {}
         for m in range(first, B * PIECES):
-            in_slot[N_CHUNKS * (1 + m - first) + 1] = m
+            in_slot[N_CHUNKS * (m - first) + FIRST_SLOT] = m
 
         last = UNITS - 1
+        for m in range(first, first + 1):
+            regroup_x(on_gpsimd, m, 0, G_SHARE)
         for slot in range(N_CHUNKS * UNITS + LAG):
             u, g = divmod(slot, N_CHUNKS)
             if u < UNITS:
@@ -354,22 +379,24 @@ def tile_channelattention_pa_t_kernel(tc, x, w_q, w_k, temperature, out):
             if k == 3 and v == last:
                 quantise(v, 2, 3)
                 quantise(v, 3, 4)
-            if slot in in_slot:
-                regroup_x(on_scalar, in_slot[slot], V_SHARE, HALF)
-            if slot - 1 in in_slot:
-                regroup_x(on_vector, in_slot[slot - 1], 0, V_SHARE)
-            if slot - 2 in in_slot:
-                regroup_x(on_scalar, in_slot[slot - 2], HALF, PIECE)
             if slot - 4 in in_slot:
                 quantise_x(in_slot[slot - 4])
-            if k == SCORES_AT and is_pair(v - 1):
-                scores(v - 1)
-            if k == SCALE_AT and is_pair(v - 1):
-                scale_scores(v - 1)
+            if slot + 4 in in_slot and G_SHARE > 0:
+                regroup_x(on_gpsimd, in_slot[slot + 4], 0, G_SHARE)
+            if slot in in_slot:
+                regroup_x(on_scalar, in_slot[slot], G_SHARE + V_SHARE, PIECE)
+            if slot - 1 in in_slot and V_SHARE > 0:
+                regroup_x(on_vector, in_slot[slot - 1], G_SHARE, G_SHARE + V_SHARE)
+            w, r = divmod(slot - LAG - SCORES_AT, N_CHUNKS)
+            if r == 0 and is_pair(w) and w < last:
+                scores(w)
+            w, r = divmod(slot - LAG - SCALE_AT, N_CHUNKS)
+            if r == 0 and is_pair(w) and w < last:
+                scale_scores(w)
             if slot == N_CHUNKS * last + INVERT_AT:
                 for head in range(HEADS - 2):
                     exponentials(head)
-            if slot == N_CHUNKS * last + LAG:
+            if slot == N_CHUNKS * last + LAG + 2:
                 exponentials(HEADS - 2)
 
         scores(last)

@@ -19,12 +19,15 @@ N_CHUNKS = N // CHUNK
 FIRST = 128
 PIECE = 256
 PIECES = N // PIECE
-G_SHARE = 128
+G_SHARE = 160
 V_SHARE = 0
 HEAD_PIECES = 2
 FIRST_LATER = PIECES + HEAD_PIECES
-FIRST_SLOT = 5
+FIRST_SLOT, DENSE, N_DENSE = 6, 4, 0
+QX_AT = 3
 X_BUFS = 2
+BY_SCALAR = 14
+GROUP = 4
 SUM_AT, SPREAD_AT, INVERT_AT = 4, 6, 6
 QUANTISE_AT = 0
 SUM_BANKS, MUL_BANKS = 4, 4
@@ -83,8 +86,8 @@ def tile_channelattention_pa_t_kernel(tc, x, w_q, w_k, temperature, out):
         w_rows = [w.rearrange("(p j) o -> p j o", j=PACK) for w in (w_q, w_k)]
         nc.sync.dma_start(out=w_first[:], in_=w_rows[0][:, :, 0:FIRST])
         load_x(0)
-        nc.sync.dma_start(out=w_raw[0][:, :, FIRST:C], in_=w_rows[0][:, :, FIRST:C])
         nc.sync.dma_start(out=w_raw[1][:], in_=w_rows[1])
+        nc.sync.dma_start(out=w_raw[0][:, :, FIRST:C], in_=w_rows[0][:, :, FIRST:C])
         for b in range(1, B):
             load_x(b)
 
@@ -123,10 +126,10 @@ def tile_channelattention_pa_t_kernel(tc, x, w_q, w_k, temperature, out):
                 op1=ALU.add,
             )
 
-        def regroup_w(s, h0, h1):
+        def regroup_w(copy, s, h0, h1):
             cols = slice(h0 * D, h1 * D)
             rows = w_first if s == 0 and h1 * D <= FIRST else w_raw[s]
-            on_vector(w_grouped[s][:, cols, :], rows[:, :, cols])
+            copy(w_grouped[s][:, cols, :], rows[:, :, cols])
 
         def quantise_w(s, h0, h1):
             cols = slice(h0 * D, h1 * D)
@@ -210,9 +213,9 @@ def tile_channelattention_pa_t_kernel(tc, x, w_q, w_k, temperature, out):
 
         def normalise(u, g):
             b, h, s = unit_of(u)
-            if g == 0:
-                normed[u] = units.tile(
-                    [P, N_CHUNKS, D, PACK], BF16, name="normed", align_bytes=64
+            if s == 0 and g == 0:
+                normed[u // 2] = units.tile(
+                    [P, 2, N_CHUNKS, D, PACK], BF16, name="normed", bufs=3, align_bytes=64
                 )
             chans = slice(h * D, (h + 1) * D)
             bank = mul_banks.tile([P, PACK, D], F32, name="mul_bank")
@@ -228,7 +231,7 @@ def tile_channelattention_pa_t_kernel(tc, x, w_q, w_k, temperature, out):
                     stop=True,
                 )
             nc.vector.scalar_tensor_tensor(
-                out=normed[u][:, g, :, :],
+                out=normed[u // 2][:, s, g, :, :],
                 in0=inv_norm_row[u][:].unsqueeze(2).to_broadcast([P, D, PACK]),
                 scalar=1.0 / EPS,
                 in1=bank[:].rearrange("p t o -> p o t"),
@@ -236,14 +239,15 @@ def tile_channelattention_pa_t_kernel(tc, x, w_q, w_k, temperature, out):
                 op1=ALU.mult,
             )
 
-        def quantise(u, g0=0, g1=N_CHUNKS):
-            if g0 == 0:
-                codes[u] = words.tile([P, N_CHUNKS, D], U32, name="codes", align_bytes=64)
-                scales[u] = words.tile([P, N_CHUNKS, D], U8, name="scales", align_bytes=64)
+        def quantise(head, first, last):
+            if first == 0:
+                codes[head] = words.tile([P, 2 * N_CHUNKS, D], U32, name="codes", align_bytes=64)
+                scales[head] = words.tile([P, 2 * N_CHUNKS, D], U8, name="scales", align_bytes=64)
+            flat = normed[head][:].rearrange("p s g o t -> p (s g) (o t)")
             nc.vector.quantize_mx(
-                out=codes[u][:, g0:g1, :].rearrange("p g o -> p (g o)").bitcast(FP8X4),
-                scales=scales[u][:, g0:g1, :].rearrange("p g o -> p (g o)"),
-                in_=normed[u][:, g0:g1, :, :].rearrange("p g o t -> p (g o t)"),
+                out=codes[head][:, first:last, :].rearrange("p g o -> p (g o)").bitcast(FP8X4),
+                scales=scales[head][:, first:last, :].rearrange("p g o -> p (g o)"),
+                in_=flat[:, first:last, :].rearrange("p g c -> p (g c)"),
             )
 
         HEADS = B * NH
@@ -257,21 +261,33 @@ def tile_channelattention_pa_t_kernel(tc, x, w_q, w_k, temperature, out):
         score_bank = {}
 
         def scores(pair):
-            bank = mul_banks.tile([P, PACK, D], F32, name="mul_bank")
-            score_bank[pair] = bank[:, 0, :]
+            if pair // 2 < BY_SCALAR:
+                bank = sum_banks.tile([P, CHUNK], F32, name="sum_bank")
+                score_bank[pair] = bank[:, 0:D]
+            else:
+                bank = mul_banks.tile([P, PACK, D], F32, name="mul_bank")
+                score_bank[pair] = bank[:, 0, :]
             for g in range(N_CHUNKS):
                 nc.tensor.matmul_mx(
                     out=score_bank[pair],
-                    lhsT=codes[pair - 1][:, g, :].bitcast(FP8X4),
-                    lhsT_scale=scales[pair - 1][:, g, :],
-                    rhs=codes[pair][:, g, :].bitcast(FP8X4),
-                    rhs_scale=scales[pair][:, g, :],
+                    lhsT=codes[pair // 2][:, g, :].bitcast(FP8X4),
+                    lhsT_scale=scales[pair // 2][:, g, :],
+                    rhs=codes[pair // 2][:, N_CHUNKS + g, :].bitcast(FP8X4),
+                    rhs_scale=scales[pair // 2][:, N_CHUNKS + g, :],
                     start=(g == 0),
                     stop=(g == N_CHUNKS - 1),
                 )
 
         def scale_scores(pair):
             h = unit_of(pair)[1]
+            if pair // 2 < BY_SCALAR:
+                nc.scalar.activation(
+                    out=neg_a[:, pair // 2, :],
+                    in_=score_bank[pair],
+                    func=ACT.Copy,
+                    scale=neg_temp[:, h : h + 1],
+                )
+                return
             nc.vector.tensor_scalar(
                 out=neg_a[:, pair // 2, :],
                 in0=score_bank[pair],
@@ -280,6 +296,14 @@ def tile_channelattention_pa_t_kernel(tc, x, w_q, w_k, temperature, out):
                 op0=ALU.mult,
                 op1=ALU.min,
                 accum_out=neg_max[:, pair // 2 : pair // 2 + 1],
+            )
+
+        def minima(h0, h1):
+            nc.vector.tensor_reduce(
+                out=neg_max[:, h0:h1],
+                in_=neg_a[:, h0:h1, :],
+                axis=mybir.AxisListType.X,
+                op=ALU.min,
             )
 
         def exponentials(head):
@@ -314,7 +338,7 @@ def tile_channelattention_pa_t_kernel(tc, x, w_q, w_k, temperature, out):
             return 0 <= u < UNITS and u % 2 == 1
 
 
-        regroup_w(0, 0, 1)
+        regroup_w(on_vector, 0, 0, 1)
         regroup_x(on_vector, 0)
         regroup_x(on_scalar, 1)
         quantise_w(0, 0, 1)
@@ -331,30 +355,32 @@ def tile_channelattention_pa_t_kernel(tc, x, w_q, w_k, temperature, out):
         regroup_x(on_scalar, 7)
         quantise_x(5)
         quantise_x(6)
-        regroup_w(1, 0, 1)
         quantise_x(7)
 
-        regroup_w(0, 1, NH)
+        regroup_w(on_vector, 1, 0, 1)
+        regroup_w(on_vector, 1, 1, NH)
         quantise_w(1, 0, 1)
-        regroup_w(1, 1, NH)
+        regroup_w(on_vector, 0, 1, NH)
+        quantise_w(1, 1, 2)
         quantise_w(0, 1, 2)
         quantise_w(0, 2, NH)
-        quantise_w(1, 1, 2)
         quantise_w(1, 2, NH)
 
         for m in range(PIECES, PIECES + HEAD_PIECES):
             regroup_x(on_vector, m)
             if m > PIECES:
                 quantise_x(m - 1)
-        quantise_x(PIECES + HEAD_PIECES - 1)
+        if HEAD_PIECES > 0:
+            quantise_x(PIECES + HEAD_PIECES - 1)
 
         first = PIECES + HEAD_PIECES
         in_slot = {}
         for m in range(first, B * PIECES):
-            in_slot[N_CHUNKS * (m - first) + FIRST_SLOT] = m
+            i = m - first
+            in_slot[FIRST_SLOT + (DENSE * i if i < N_DENSE else DENSE * N_DENSE + N_CHUNKS * (i - N_DENSE))] = m
 
         last = UNITS - 1
-        for m in range(first, first + 1):
+        for m in range(first, first + 2):
             regroup_x(on_gpsimd, m, 0, G_SHARE)
         for slot in range(N_CHUNKS * UNITS + LAG):
             u, g = divmod(slot, N_CHUNKS)
@@ -372,18 +398,21 @@ def tile_channelattention_pa_t_kernel(tc, x, w_q, w_k, temperature, out):
             w, r = divmod(slot - INVERT_AT, N_CHUNKS)
             if r == 0 and 0 <= w < UNITS:
                 invert_norm(w)
-            if k == QUANTISE_AT and 0 <= v - 1 < last:
-                quantise(v - 1)
+            if k == QUANTISE_AT and is_pair(v - 1) and v - 1 < last:
+                quantise(v // 2 - 1, 0, 2 * N_CHUNKS)
+            if k == QUANTISE_AT and v == last:
+                quantise(v // 2, 0, N_CHUNKS)
             if k == 2 and v == last:
-                quantise(v, 0, 2)
+                quantise(v // 2, N_CHUNKS, N_CHUNKS + 2)
             if k == 3 and v == last:
-                quantise(v, 2, 3)
-                quantise(v, 3, 4)
-            if slot - 4 in in_slot:
-                quantise_x(in_slot[slot - 4])
-            if slot + 4 in in_slot and G_SHARE > 0:
-                regroup_x(on_gpsimd, in_slot[slot + 4], 0, G_SHARE)
-            if slot in in_slot:
+                quantise(v // 2, N_CHUNKS + 2, N_CHUNKS + 3)
+                quantise(v // 2, N_CHUNKS + 3, 2 * N_CHUNKS)
+            if slot - QX_AT in in_slot:
+                m = in_slot[slot - QX_AT]
+                quantise_x(m)
+                if m + 2 < B * PIECES:
+                    regroup_x(on_gpsimd, m + 2, 0, G_SHARE)
+            if slot in in_slot and G_SHARE + V_SHARE < PIECE:
                 regroup_x(on_scalar, in_slot[slot], G_SHARE + V_SHARE, PIECE)
             if slot - 1 in in_slot and V_SHARE > 0:
                 regroup_x(on_vector, in_slot[slot - 1], G_SHARE, G_SHARE + V_SHARE)
@@ -393,6 +422,9 @@ def tile_channelattention_pa_t_kernel(tc, x, w_q, w_k, temperature, out):
             w, r = divmod(slot - LAG - SCALE_AT, N_CHUNKS)
             if r == 0 and is_pair(w) and w < last:
                 scale_scores(w)
+            w, r = divmod(slot - LAG - SCALE_AT - 2, N_CHUNKS)
+            if r == 0 and is_pair(w) and (w // 2 + 1 == BY_SCALAR or (w // 2 + 1) % GROUP == 0) and w // 2 < BY_SCALAR:
+                minima(w // 2 // GROUP * GROUP, w // 2 + 1)
             if slot == N_CHUNKS * last + INVERT_AT:
                 for head in range(HEADS - 2):
                     exponentials(head)

from contextlib import ExitStack

import concourse.mybir as mybir
from concourse.masks import make_identity

F32 = mybir.dt.float32
BF16 = mybir.dt.bfloat16
U32 = mybir.dt.uint32
U8 = mybir.dt.uint8
FP8X4 = mybir.dt.float8_e4m3fn_x4
ACT = mybir.ActivationFunctionType
ALU = mybir.AluOpType

P = 128
PACK = 4
B, C, NH, D, N = 4, 512, 4, 128, 2048
CHUNK = P * PACK
N_CHUNKS = N // CHUNK
FIRST = 128
PIECE = 256
PIECES = N // PIECE
G_SHARE = 160
V_SHARE = 0
HEAD_PIECES = 2
FIRST_LATER = PIECES + HEAD_PIECES
FIRST_SLOT, DENSE, N_DENSE = 6, 4, 0
QX_AT = 3
X_BUFS = 2
BY_SCALAR = 14
GROUP = 4
SUM_AT, SPREAD_AT, INVERT_AT = 4, 6, 6
QUANTISE_AT = 0
SUM_BANKS, MUL_BANKS = 4, 4
SCORES_AT, SCALE_AT = 8, 9
LAG = 8
RUN = 4
UNITS = B * NH * 2
EPS = 1e-12

FLOPS = 2 * B * N * C * (2 * C) + 2 * B * NH * D * D * N


def unit_of(u):
    b, rest = divmod(u, NH * 2)
    h, s = divmod(rest, 2)
    return b, h, s


def regroup(copy, grouped, rows):
    copy(
        out=grouped.rearrange("p (c i) j -> p c j i", i=RUN),
        in_=rows.rearrange("p j (c i) -> p c j i", i=RUN),
    )


def tile_channelattention_pa_t_kernel(tc, x, w_q, w_k, temperature, out):
    nc = tc.nc
    x_rows = x.rearrange("b (p j) w h z -> b p j (w h z)", j=PACK)

    with ExitStack() as stack:
        stack.enter_context(tc.manual_schedule())
        keep = stack.enter_context(tc.tile_pool(name="keep", bufs=1))
        head = stack.enter_context(tc.tile_pool(name="head", bufs=4))
        stage = stack.enter_context(tc.tile_pool(name="stage", bufs=X_BUFS))
        units = stack.enter_context(tc.tile_pool(name="units", bufs=3))
        words = stack.enter_context(tc.tile_pool(name="words", bufs=4))
        sum_banks = stack.enter_context(tc.psum_pool(name="sum_banks", bufs=SUM_BANKS))
        mul_banks = stack.enter_context(tc.psum_pool(name="mul_banks", bufs=MUL_BANKS))

        w_raw = [keep.tile([P, PACK, C], BF16, name="w_raw%d" % s) for s in range(2)]
        w_first = keep.tile([P, PACK, FIRST], BF16, name="w_first")
        x_raw = [
            [keep.tile([P, PACK, CHUNK], BF16, name="x_raw%d_%d" % (b, g)) for g in range(N_CHUNKS)]
            for b in range(B)
        ]
        temp_bf = keep.tile([P, NH], BF16, name="temp_bf")

        def load_x(b):
            for g in range(N_CHUNKS):
                cols = slice(g * CHUNK, (g + 1) * CHUNK)
                nc.sync.dma_start(out=x_raw[b][g][:], in_=x_rows[b][:, :, cols])

        nc.scalar.dma_start(
            out=temp_bf[:], in_=temperature.rearrange("h a c -> (h a c)").partition_broadcast(P)
        )
        w_rows = [w.rearrange("(p j) o -> p j o", j=PACK) for w in (w_q, w_k)]
        nc.sync.dma_start(out=w_first[:], in_=w_rows[0][:, :, 0:FIRST])
        load_x(0)
        nc.sync.dma_start(out=w_raw[1][:], in_=w_rows[1])
        nc.sync.dma_start(out=w_raw[0][:, :, FIRST:C], in_=w_rows[0][:, :, FIRST:C])
        for b in range(1, B):
            load_x(b)

        ident = keep.tile([P, P], F32, name="ident")
        make_identity(nc, ident[:])
        neg_temp = keep.tile([P, NH], F32, name="neg_temp")
        nc.gpsimd.tensor_scalar(
            out=neg_temp[:], in0=temp_bf[:], scalar1=-1.0, scalar2=0.0, op0=ALU.mult, op1=ALU.add
        )
        warm = keep.tile([P, 1], F32, name="warm")
        nc.vector.memset(warm[:], 1.0)
        nc.scalar.activation(out=warm[:], in_=warm[:], func=ACT.Abs_reciprocal_sqrt)

        w_codes = keep.tile([P, 2, C], U32, name="w_codes", align_bytes=64)
        w_scales = keep.tile([P, 2, C], U8, name="w_scales", align_bytes=64)
        x_codes = [keep.tile([P, N], U32, name="x_codes%d" % b, align_bytes=64) for b in range(B)]
        x_scales = [keep.tile([P, N], U8, name="x_scales%d" % b, align_bytes=64) for b in range(B)]

        w_grouped = [
            keep.tile([P, C, PACK], BF16, name="w_grouped%d" % s, align_bytes=64) for s in range(2)
        ]

        def on_vector(grouped, rows):
            regroup(nc.vector.tensor_copy, grouped, rows)

        def on_scalar(grouped, rows):
            regroup(nc.scalar.copy, grouped, rows)

        def on_gpsimd(grouped, rows):
            nc.gpsimd.tensor_scalar(
                out=grouped,
                in0=rows.rearrange("p j w -> p w j"),
                scalar1=1.0,
                scalar2=0.0,
                op0=ALU.mult,
                op1=ALU.add,
            )

        def regroup_w(copy, s, h0, h1):
            cols = slice(h0 * D, h1 * D)
            rows = w_first if s == 0 and h1 * D <= FIRST else w_raw[s]
            copy(w_grouped[s][:, cols, :], rows[:, :, cols])

        def quantise_w(s, h0, h1):
            cols = slice(h0 * D, h1 * D)
            nc.vector.quantize_mx(
                out=w_codes[:, s, cols].bitcast(FP8X4),
                scales=w_scales[:, s, cols],
                in_=w_grouped[s][:, cols, :].rearrange("p o j -> p (o j)"),
            )

        x_grouped = {}

        def regroup_x(copy, m, first=0, last=PIECE):
            b, piece = divmod(m, PIECES)
            if m not in x_grouped:
                if m < FIRST_LATER:
                    x_grouped[m] = head.tile([P, PIECE, PACK], BF16, name="x_head", align_bytes=64)
                else:
                    x_grouped[m] = stage.tile(
                        [P, PIECE, PACK], BF16, name="x_grouped", align_bytes=64
                    )
            g, start = divmod(piece * PIECE, CHUNK)
            cols = slice(start + first, start + last)
            copy(x_grouped[m][:, first:last, :], x_raw[b][g][:, :, cols])

        def quantise_x(m):
            b, piece = divmod(m, PIECES)
            cols = slice(piece * PIECE, (piece + 1) * PIECE)
            nc.vector.quantize_mx(
                out=x_codes[b][:, cols].bitcast(FP8X4),
                scales=x_scales[b][:, cols],
                in_=x_grouped[m][:].rearrange("p n j -> p (n j)"),
            )

        square_sum = {}
        total = {}
        inv_norm_row = {}
        normed = {}
        codes = {}
        scales = {}

        def sum_squares(u, g):
            b, h, s = unit_of(u)
            if g == 0:
                square_sum[u] = units.tile([P, N_CHUNKS], F32, name="square_sum")
            chans = slice(h * D, (h + 1) * D)
            toks = slice(g * CHUNK, (g + 1) * CHUNK)
            bank = sum_banks.tile([P, CHUNK], F32, name="sum_bank")
            nc.tensor.matmul_mx(
                out=bank[:],
                lhsT=w_codes[:, s, chans].bitcast(FP8X4),
                lhsT_scale=w_scales[:, s, chans],
                rhs=x_codes[b][:, toks].bitcast(FP8X4),
                rhs_scale=x_scales[b][:, toks],
                start=True,
                stop=True,
            )
            squares = units.tile([P, CHUNK], BF16, name="squares", bufs=2)
            nc.scalar.activation(
                out=squares[:], in_=bank[:], func=ACT.Square, accum_out=square_sum[u][:, g : g + 1]
            )

        def add_squares(u):
            sums = units.tile([P, N_CHUNKS], F32, name="sums")
            total[u] = units.tile([P, 1], F32, name="total")
            nc.scalar.activation(
                out=sums[:], in_=square_sum[u][:], func=ACT.Copy, accum_out=total[u][:]
            )

        row_bank = {}

        def spread_sum(u):
            bank = sum_banks.tile([P, CHUNK], F32, name="sum_bank")
            row_bank[u] = bank[:, 0:D]
            nc.tensor.transpose(row_bank[u], total[u][:, 0:1].to_broadcast([P, P]), ident[:])

        def invert_norm(u):
            inv_norm_row[u] = units.tile([P, D], F32, name="inv_norm_row")
            nc.scalar.activation(
                out=inv_norm_row[u][:], in_=row_bank[u], func=ACT.Abs_reciprocal_sqrt
            )

        def normalise(u, g):
            b, h, s = unit_of(u)
            if s == 0 and g == 0:
                normed[u // 2] = units.tile(
                    [P, 2, N_CHUNKS, D, PACK], BF16, name="normed", bufs=3, align_bytes=64
                )
            chans = slice(h * D, (h + 1) * D)
            bank = mul_banks.tile([P, PACK, D], F32, name="mul_bank")
            for t in range(PACK):
                toks = slice(g * CHUNK + t * P, g * CHUNK + (t + 1) * P)
                nc.tensor.matmul_mx(
                    out=bank[:, t, :],
                    lhsT=x_codes[b][:, toks].bitcast(FP8X4),
                    lhsT_scale=x_scales[b][:, toks],
                    rhs=w_codes[:, s, chans].bitcast(FP8X4),
                    rhs_scale=w_scales[:, s, chans],
                    start=True,
                    stop=True,
                )
            nc.vector.scalar_tensor_tensor(
                out=normed[u // 2][:, s, g, :, :],
                in0=inv_norm_row[u][:].unsqueeze(2).to_broadcast([P, D, PACK]),
                scalar=1.0 / EPS,
                in1=bank[:].rearrange("p t o -> p o t"),
                op0=ALU.min,
                op1=ALU.mult,
            )

        def quantise(head, first, last):
            if first == 0:
                codes[head] = words.tile([P, 2 * N_CHUNKS, D], U32, name="codes", align_bytes=64)
                scales[head] = words.tile([P, 2 * N_CHUNKS, D], U8, name="scales", align_bytes=64)
            flat = normed[head][:].rearrange("p s g o t -> p (s g) (o t)")
            nc.vector.quantize_mx(
                out=codes[head][:, first:last, :].rearrange("p g o -> p (g o)").bitcast(FP8X4),
                scales=scales[head][:, first:last, :].rearrange("p g o -> p (g o)"),
                in_=flat[:, first:last, :].rearrange("p g c -> p (g c)"),
            )

        HEADS = B * NH
        neg_a = keep.tile([P, HEADS, D], F32, name="neg_a")
        neg_max = keep.tile([P, HEADS], F32, name="neg_max")
        e = keep.tile([P, HEADS, D], F32, name="e")
        e_sum = keep.tile([P, HEADS], F32, name="e_sum")
        inv_sum = keep.tile([P, HEADS], F32, name="inv_sum")
        prob = keep.tile([P, HEADS, D], F32, name="prob")

        score_bank = {}

        def scores(pair):
            if pair // 2 < BY_SCALAR:
                bank = sum_banks.tile([P, CHUNK], F32, name="sum_bank")
                score_bank[pair] = bank[:, 0:D]
            else:
                bank = mul_banks.tile([P, PACK, D], F32, name="mul_bank")
                score_bank[pair] = bank[:, 0, :]
            for g in range(N_CHUNKS):
                nc.tensor.matmul_mx(
                    out=score_bank[pair],
                    lhsT=codes[pair // 2][:, g, :].bitcast(FP8X4),
                    lhsT_scale=scales[pair // 2][:, g, :],
                    rhs=codes[pair // 2][:, N_CHUNKS + g, :].bitcast(FP8X4),
                    rhs_scale=scales[pair // 2][:, N_CHUNKS + g, :],
                    start=(g == 0),
                    stop=(g == N_CHUNKS - 1),
                )

        def scale_scores(pair):
            h = unit_of(pair)[1]
            if pair // 2 < BY_SCALAR:
                nc.scalar.activation(
                    out=neg_a[:, pair // 2, :],
                    in_=score_bank[pair],
                    func=ACT.Copy,
                    scale=neg_temp[:, h : h + 1],
                )
                return
            nc.vector.tensor_scalar(
                out=neg_a[:, pair // 2, :],
                in0=score_bank[pair],
                scalar1=neg_temp[:, h : h + 1],
                scalar2=None,
                op0=ALU.mult,
                op1=ALU.min,
                accum_out=neg_max[:, pair // 2 : pair // 2 + 1],
            )

        def minima(h0, h1):
            nc.vector.tensor_reduce(
                out=neg_max[:, h0:h1],
                in_=neg_a[:, h0:h1, :],
                axis=mybir.AxisListType.X,
                op=ALU.min,
            )

        def exponentials(head):
            nc.scalar.activation(
                out=e[:, head, :],
                in_=neg_a[:, head, :],
                func=ACT.Exp,
                scale=-1.0,
                bias=neg_max[:, head : head + 1],
                accum_out=e_sum[:, head : head + 1],
            )

        def invert_sums(h0, h1):
            nc.vector.reciprocal(out=inv_sum[:, h0:h1], in_=e_sum[:, h0:h1])

        def divide(head):
            nc.vector.tensor_scalar(
                out=prob[:, head, :],
                in0=e[:, head, :],
                scalar1=inv_sum[:, head : head + 1],
                scalar2=None,
                op0=ALU.mult,
            )

        def store(h0, h1):
            b, h = divmod(h0, NH)
            nc.sync.dma_start(
                out=out[b, h : h + h1 - h0].rearrange("h i j -> i h j"), in_=prob[:, h0:h1, :]
            )

        def is_pair(u):
            return 0 <= u < UNITS and u % 2 == 1


        regroup_w(on_vector, 0, 0, 1)
        regroup_x(on_vector, 0)
        regroup_x(on_scalar, 1)
        quantise_w(0, 0, 1)
        quantise_x(0)
        regroup_x(on_vector, 2)
        regroup_x(on_scalar, 3)
        quantise_x(1)
        quantise_x(2)
        regroup_x(on_vector, 4)
        regroup_x(on_scalar, 5)
        quantise_x(3)
        quantise_x(4)
        regroup_x(on_vector, 6)
        regroup_x(on_scalar, 7)
        quantise_x(5)
        quantise_x(6)
        quantise_x(7)

        regroup_w(on_vector, 1, 0, 1)
        regroup_w(on_vector, 1, 1, NH)
        quantise_w(1, 0, 1)
        regroup_w(on_vector, 0, 1, NH)
        quantise_w(1, 1, 2)
        quantise_w(0, 1, 2)
        quantise_w(0, 2, NH)
        quantise_w(1, 2, NH)

        for m in range(PIECES, PIECES + HEAD_PIECES):
            regroup_x(on_vector, m)
            if m > PIECES:
                quantise_x(m - 1)
        if HEAD_PIECES > 0:
            quantise_x(PIECES + HEAD_PIECES - 1)

        first = PIECES + HEAD_PIECES
        in_slot = {}
        for m in range(first, B * PIECES):
            i = m - first
            in_slot[FIRST_SLOT + (DENSE * i if i < N_DENSE else DENSE * N_DENSE + N_CHUNKS * (i - N_DENSE))] = m

        last = UNITS - 1
        for m in range(first, first + 2):
            regroup_x(on_gpsimd, m, 0, G_SHARE)
        for slot in range(N_CHUNKS * UNITS + LAG):
            u, g = divmod(slot, N_CHUNKS)
            if u < UNITS:
                sum_squares(u, g)
            w, r = divmod(slot - SUM_AT, N_CHUNKS)
            if r == 0 and 0 <= w < UNITS:
                add_squares(w)
            v, k = divmod(slot - LAG, N_CHUNKS)
            if 0 <= v < UNITS:
                normalise(v, k)
            w, r = divmod(slot - SPREAD_AT, N_CHUNKS)
            if r == 0 and 0 <= w < UNITS:
                spread_sum(w)
            w, r = divmod(slot - INVERT_AT, N_CHUNKS)
            if r == 0 and 0 <= w < UNITS:
                invert_norm(w)
            if k == QUANTISE_AT and is_pair(v - 1) and v - 1 < last:
                quantise(v // 2 - 1, 0, 2 * N_CHUNKS)
            if k == QUANTISE_AT and v == last:
                quantise(v // 2, 0, N_CHUNKS)
            if k == 2 and v == last:
                quantise(v // 2, N_CHUNKS, N_CHUNKS + 2)
            if k == 3 and v == last:
                quantise(v // 2, N_CHUNKS + 2, N_CHUNKS + 3)
                quantise(v // 2, N_CHUNKS + 3, 2 * N_CHUNKS)
            if slot - QX_AT in in_slot:
                m = in_slot[slot - QX_AT]
                quantise_x(m)
                if m + 2 < B * PIECES:
                    regroup_x(on_gpsimd, m + 2, 0, G_SHARE)
            if slot in in_slot and G_SHARE + V_SHARE < PIECE:
                regroup_x(on_scalar, in_slot[slot], G_SHARE + V_SHARE, PIECE)
            if slot - 1 in in_slot and V_SHARE > 0:
                regroup_x(on_vector, in_slot[slot - 1], G_SHARE, G_SHARE + V_SHARE)
            w, r = divmod(slot - LAG - SCORES_AT, N_CHUNKS)
            if r == 0 and is_pair(w) and w < last:
                scores(w)
            w, r = divmod(slot - LAG - SCALE_AT, N_CHUNKS)
            if r == 0 and is_pair(w) and w < last:
                scale_scores(w)
            w, r = divmod(slot - LAG - SCALE_AT - 2, N_CHUNKS)
            if r == 0 and is_pair(w) and (w // 2 + 1 == BY_SCALAR or (w // 2 + 1) % GROUP == 0) and w // 2 < BY_SCALAR:
                minima(w // 2 // GROUP * GROUP, w // 2 + 1)
            if slot == N_CHUNKS * last + INVERT_AT:
                for head in range(HEADS - 2):
                    exponentials(head)
            if slot == N_CHUNKS * last + LAG + 2:
                exponentials(HEADS - 2)

        scores(last)
        invert_sums(0, HEADS - 1)
        for head in range(2 * NH):
            divide(head)
        store(0, NH)
        store(NH, 2 * NH)
        scale_scores(last)
        exponentials(HEADS - 1)
        for head in range(2 * NH, 3 * NH):
            divide(head)
        store(2 * NH, 3 * NH)
        invert_sums(HEADS - 1, HEADS)
        divide(HEADS - 1)
        store(HEADS - 1, HEADS)
        for head in range(3 * NH, HEADS - 1):
            divide(head)
        store(3 * NH, HEADS - 1)
